import numpy as np
import ml_dtypes


def mxq(x, axis, fmt="e4m3"):
    dtype, down = {"e4m3": (ml_dtypes.float8_e4m3fn, 7), "e5m2": (ml_dtypes.float8_e5m2, 14)}[fmt]
    v = np.moveaxis(np.asarray(x, np.float32).astype(ml_dtypes.bfloat16).astype(np.float64), axis, -1)
    blocks = v.reshape(v.shape[:-1] + (-1, 32))
    amax = np.abs(blocks).max(-1, keepdims=True)
    byte = np.maximum(np.where(amax > 0, np.frexp(amax)[1] - 1 + 127, 0) - down, 1)
    scale = np.exp2(byte - 127.0)
    codes = (blocks / scale).astype(np.float32).astype(dtype).astype(np.float64)
    return np.moveaxis((codes * scale).reshape(v.shape), -1, axis)


WIDE = False


def mx_kscale(k):
    if not WIDE:
        return np.ones(k)
    levels = np.array([10, -10, 5, -5, 0])
    if k % 512:
        return np.exp2(np.random.permutation(np.resize(levels, k // 32))).repeat(32)
    a = np.empty((k // 512, 16))
    for p in range(k // 512):
        a[p, :8] = np.random.permutation(np.resize(levels, 8))
        for g in range(8):
            far = levels[np.abs(levels - a[p, g]) >= 10]
            a[p, g + 8] = far[np.random.randint(len(far))]
    return np.exp2(a.ravel()).repeat(32)


BF16 = ml_dtypes.bfloat16


def bf(x):
    return np.asarray(x, np.float32).astype(BF16)


def f64(x):
    return np.asarray(x).astype(np.float64)


B, L, D, H = 1, 1024, 512, 8


def setup_inputs():
    s = mx_kscale(D)
    return {"x": bf(np.random.standard_normal((B, L, D)) * s),
            "w": bf(np.random.standard_normal((H, D, D)) / np.sqrt(D) / s[:, None] * s[None, :])}


def reference(x, w):
    wq = mxq(f64(w), 1, "e4m3")
    xq = mxq(f64(x), 2, "e4m3")
    xs = f64(bf(xq[None] @ wq[:, None])).reshape(H * B, L, D)
    return mxq(xs, 2, "e4m3") @ wq

@@ -1,0 +1,255 @@
+from contextlib import ExitStack
+
+import concourse.mybir as mybir
+from concourse.masks import make_identity
+
+H, L, D = 8, 1024, 512
+FLOPS = 2 * 2 * H * L * D * D
+
+F32 = mybir.dt.float32
+BF16 = mybir.dt.bfloat16
+U32 = mybir.dt.uint32
+U8 = mybir.dt.uint8
+FP8X4 = mybir.dt.float8_e4m3fn_x4
+
+P = 128
+PACK = 4
+LT = L // P
+BANK_DT = BF16
+
+SKEW = 7
+QC = 4
+DQ = 1
+SCALAR_NUM, SCALAR_DEN = 11, 16
+TAIL_FROM = 112
+W_COPY_AHEAD = 10
+W_SLICES = 4
+W_QUANT_AHEAD = 4
+STORE_CHUNKS = 2
+LAST_STORES = {1: 0, 3: 2, 5: 4, 6: 6, 7: 7}
+
+
+def tile_multiheadattention_pa_kernel(tc, x, w, out):
+    nc = tc.nc
+    x_rows = x.flatten_outer_dims().rearrange("(p a) k -> p a k", a=LT)
+    w_rows = w.flatten_outer_dims()
+    out_rows = out.flatten_outer_dims()
+
+    with ExitStack() as ctx:
+        consts = ctx.enter_context(tc.tile_pool(name="consts", bufs=1))
+        w_pool = ctx.enter_context(tc.tile_pool(name="w_pool", bufs=H))
+        wg_pool = ctx.enter_context(tc.tile_pool(name="wg_pool", bufs=2))
+        xs_pool = ctx.enter_context(tc.tile_pool(name="xs_pool", bufs=3))
+        o_pool = ctx.enter_context(tc.tile_pool(name="o_pool", bufs=3))
+        psum = ctx.enter_context(tc.psum_pool(name="psum", bufs=4))
+
+        warm_in = consts.tile([P, 1], F32, name="warm_in")
+        warm_out = consts.tile([P, 1], F32, name="warm_out")
+        nc.vector.memset(warm_in[:], 0.0)
+        nc.scalar.copy(out=warm_out[:], in_=warm_in[:])
+
+        ident = consts.tile([P, P], F32, name="ident")
+        make_identity(nc, ident[:])
+
+        x_sb = consts.tile([P, LT, D], BF16, name="x_sb")
+        w_raw = []
+        for h in range(H):
+            w_raw_h = w_pool.tile([P, PACK, D], BF16, name="w_raw_h", tag="w_raw")
+            w_raw.append(w_raw_h)
+
+        def load_x(a0, a1):
+            nc.sync.dma_start(out=x_sb[:, a0:a1, :], in_=x_rows[:, a0:a1, :])
+
+        def load_w(h):
+            nc.sync.dma_start(
+                out=w_raw[h][:],
+                in_=w_rows[h * D : (h + 1) * D, :].rearrange("(p j) c -> p j c", j=PACK),
+            )
+
+        load_w(0)
+        load_x(0, 2)
+        load_x(2, 4)
+        load_x(4, 8)
+        for h in range(1, H):
+            load_w(h)
+
+        w_grouped = {}
+        w_codes = {}
+        w_scales = {}
+
+        def w_views(h, t0, t1):
+            dst = w_grouped[h][:, t0 * P * PACK : t1 * P * PACK].rearrange("p (t m j) -> p m j t", t=t1 - t0, j=PACK)
+            src = w_raw[h][:].rearrange("p j (m t) -> p m j t", t=PACK)[:, :, :, t0:t1]
+            return dst, src
+
+        def w_alloc(h):
+            wg = wg_pool.tile([P, D * PACK], BF16, name="wg", tag="wg", align_bytes=64)
+            w_grouped[h] = wg
+
+        def w_copy_first():
+            w_alloc(0)
+            dst, src = w_views(0, 0, 2)
+            nc.vector.tensor_copy(out=dst, in_=src)
+            dst, src = w_views(0, 3, 4)
+            nc.scalar.copy(out=dst, in_=src)
+            dst, src = w_views(0, 2, 3)
+            nc.vector.tensor_copy(out=dst, in_=src)
+
+        def w_copy(h, t):
+            if t == 0:
+                w_alloc(h)
+            dst, src = w_views(h, t, t + W_SLICES)
+            nc.vector.tensor_copy(out=dst, in_=src)
+
+        def w_quant(h):
+            wc = w_pool.tile([P, D], U32, name="wc", tag="w_codes", align_bytes=64)
+            ws = w_pool.tile([P, D], U8, name="ws", tag="w_scales", align_bytes=64)
+            nc.vector.quantize_mx(out=wc[:].bitcast(FP8X4), scales=ws[:], in_=w_grouped[h][:])
+            w_codes[h] = wc
+            w_scales[h] = ws
+
+        x_grouped = consts.tile([P, LT, P, PACK], BF16, name="x_grouped", align_bytes=64)
+        x_codes = consts.tile([P, L], U32, name="x_codes", align_bytes=64)
+        x_scales = consts.tile([P, L], U8, name="x_scales", align_bytes=64)
+
+        def x_transpose(pr):
+            xt = psum.tile([P, 2, 2, P], F32, name="xt", tag="s1")
+            for a2 in range(2):
+                words = x_sb[:, 2 * pr + a2, :].bitcast(F32)
+                for u in range(2):
+                    nc.tensor.transpose(xt[:, a2, u, :], words[:, u : D // 2 : 2], ident[:])
+            nc.scalar.copy(
+                out=x_grouped[:, 2 * pr : 2 * pr + 2, :, :].bitcast(F32),
+                in_=xt[:].rearrange("p a u r -> p a r u"),
+            )
+
+        def x_quant(a0, a1):
+            cols = slice(P * a0, P * a1)
+            nc.vector.quantize_mx(
+                out=x_codes[:, cols].bitcast(FP8X4),
+                scales=x_scales[:, cols],
+                in_=x_grouped[:, a0:a1, :, :].rearrange("p a r j -> p (a r j)"),
+            )
+
+        xs_grouped = {}
+        xs_codes = {}
+        xs_scales = {}
+        o_sb = {}
+        banks = {}
+        accs = {}
+        reads = [0]
+
+        def psum_read(dst, src):
+            n = reads[0]
+            reads[0] = n + 1
+            if n < TAIL_FROM:
+                on_scalar = ((n + 1) * SCALAR_NUM) // SCALAR_DEN != (n * SCALAR_NUM) // SCALAR_DEN
+            else:
+                on_scalar = (n - TAIL_FROM) % 2 == 1
+            if on_scalar:
+                nc.scalar.copy(out=dst, in_=src)
+            else:
+                nc.vector.tensor_copy(out=dst, in_=src)
+
+        def stage1(h, i):
+            if i == 0:
+                xg = xs_pool.tile([P, L, PACK], BF16, name="xg", tag="xs_grouped", align_bytes=64)
+                xc = xs_pool.tile([P, L], U32, name="xc", tag="xs_codes", align_bytes=64)
+                xsc = xs_pool.tile([P, L], U8, name="xsc", tag="xs_scales", align_bytes=64)
+                xs_grouped[h] = xg
+                xs_codes[h] = xc
+                xs_scales[h] = xsc
+            bank = psum.tile([P, PACK, P], BANK_DT, name="bank", tag="s1")
+            cols = slice(i * P, (i + 1) * P)
+            for t in range(PACK):
+                chans = slice(t * P, (t + 1) * P)
+                nc.tensor.matmul_mx(
+                    out=bank[:, t, :],
+                    lhsT=w_codes[h][:, chans].bitcast(FP8X4),
+                    lhsT_scale=w_scales[h][:, chans],
+                    rhs=x_codes[:, cols].bitcast(FP8X4),
+                    rhs_scale=x_scales[:, cols],
+                    start=True,
+                    stop=True,
+                )
+            banks[(h, i)] = bank
+
+        def read_bank(h, i):
+            psum_read(xs_grouped[h][:, i * P : (i + 1) * P, :], banks[(h, i)][:].rearrange("p t l -> p l t"))
+
+        def xs_quant(h, k):
+            cols = slice(k * QC * P, (k + 1) * QC * P)
+            nc.vector.quantize_mx(
+                out=xs_codes[h][:, cols].bitcast(FP8X4),
+                scales=xs_scales[h][:, cols],
+                in_=xs_grouped[h][:, cols, :].rearrange("p l j -> p (l j)"),
+            )
+
+        def stage2(h, i):
+            if i == 0:
+                ot = o_pool.tile([P, LT, D], F32, name="ot", tag="o_sb")
+                o_sb[h] = ot
+            acc = psum.tile([P, D], F32, name="acc", tag="s2")
+            cols = slice(i * P, (i + 1) * P)
+            nc.tensor.matmul_mx(
+                out=acc[:],
+                lhsT=xs_codes[h][:, cols].bitcast(FP8X4),
+                lhsT_scale=xs_scales[h][:, cols],
+                rhs=w_codes[h][:].bitcast(FP8X4),
+                rhs_scale=w_scales[h][:],
+                start=True,
+                stop=True,
+            )
+            accs[(h, i)] = acc
+
+        def read_acc(h, i):
+            psum_read(
+                o_sb[h][:, i, :].rearrange("p (m t) -> p m t", t=PACK),
+                accs[(h, i)][:].rearrange("p (t m) -> p m t", t=PACK),
+            )
+
+        def store(h, a0, a1):
+            nc.sync.dma_start(
+                out=out_rows[h * L : (h + 1) * L, :].rearrange("(p a) e -> p a e", a=LT)[:, a0:a1, :],
+                in_=o_sb[h][:, a0:a1, :],
+            )
+
+        with tc.manual_schedule():
+            w_copy_first()
+            x_transpose(0)
+            w_quant(0)
+            x_quant(0, 2)
+            x_transpose(1)
+            x_quant(2, 4)
+
+            for g in range(H * LT + SKEW):
+                g2 = g - SKEW
+                if g < H * LT:
+                    stage1(g // LT, g % LT)
+                if g2 >= 0:
+                    stage2(g2 // LT, g2 % LT)
+                if g == 0:
+                    x_transpose(2)
+                    x_transpose(3)
+                if g < H * LT:
+                    read_bank(g // LT, g % LT)
+                if g2 >= 0:
+                    read_acc(g2 // LT, g2 % LT)
+                if g == 1:
+                    x_quant(4, 8)
+                gq = g - DQ
+                if 0 <= gq < H * LT and gq % QC == QC - 1:
+                    xs_quant(gq // LT, (gq % LT) // QC)
+                for h in range(1, H):
+                    for t in range(0, PACK, W_SLICES):
+                        if g == max(t, LT * h - W_COPY_AHEAD + t):
+                            w_copy(h, t)
+                    if g == max(5, LT * h - W_QUANT_AHEAD):
+                        w_quant(h)
+                if g2 >= 0:
+                    h2, i2 = g2 // LT, g2 % LT
+                    if h2 < H - 1:
+                        if i2 % STORE_CHUNKS == STORE_CHUNKS - 1:
+                            store(h2, i2 + 1 - STORE_CHUNKS, i2 + 1)
+                    elif i2 in LAST_STORES:
+                        store(h2, LAST_STORES[i2], i2 + 1)

@@ -31,7 +31,7 @@ LAST_STORES = {1: 0, 3: 2, 5: 4, 6: 6, 7: 7}
 
 def tile_multiheadattention_pa_kernel(tc, x, w, out):
     nc = tc.nc
-    x_rows = x.flatten_outer_dims().rearrange("(p a) k -> p a k", a=LT)
+    x_rows = x.flatten_outer_dims().rearrange("(s p e) k -> p s e k", s=LT // 2, e=2)
     w_rows = w.flatten_outer_dims()
     out_rows = out.flatten_outer_dims()
 
@@ -58,7 +58,10 @@ def tile_multiheadattention_pa_kernel(tc, x, w, out):
             w_raw.append(w_raw_h)
 
         def load_x(a0, a1):
-            nc.sync.dma_start(out=x_sb[:, a0:a1, :], in_=x_rows[:, a0:a1, :])
+            nc.sync.dma_start(
+                out=x_sb[:, a0:a1, :].rearrange("p (s e) k -> p s e k", e=2),
+                in_=x_rows[:, a0 // 2 : a1 // 2, :, :],
+            )
 
         def load_w(h):
             nc.sync.dma_start(
@@ -210,7 +213,9 @@ def tile_multiheadattention_pa_kernel(tc, x, w, out):
 
         def store(h, a0, a1):
             nc.sync.dma_start(
-                out=out_rows[h * L : (h + 1) * L, :].rearrange("(p a) e -> p a e", a=LT)[:, a0:a1, :],
+                out=out_rows[h * L : (h + 1) * L, :].rearrange("(s p e) f -> p s e f", s=LT // 2, e=2)[
+                    :, a0 // 2, a0 % 2 : a0 % 2 + a1 - a0, :
+                ],
                 in_=o_sb[h][:, a0:a1, :],
             )
 

@@ -17,15 +17,15 @@ PACK = 4
 LT = L // P
 BANK_DT = BF16
 
-SKEW = 7
-QC = 4
-DQ = 1
-SCALAR_NUM, SCALAR_DEN = 11, 16
-TAIL_FROM = 112
-W_COPY_AHEAD = 10
-W_SLICES = 4
-W_QUANT_AHEAD = 4
-STORE_CHUNKS = 2
+PAIR = 2
+NP = H * LT // PAIR
+HP = LT // PAIR
+SKEW = 3
+QP = 2
+SCALAR_NUM, SCALAR_DEN = 5, 16
+TAIL_FROM = H * LT - PAIR * SKEW
+W_COPY_AHEAD = 5
+W_QUANT_AHEAD = 2
 LAST_STORES = {1: 0, 3: 2, 5: 4, 6: 6, 7: 7}
 
 
@@ -98,10 +98,9 @@ def tile_multiheadattention_pa_kernel(tc, x, w, out):
             dst, src = w_views(0, 2, 3)
             nc.vector.tensor_copy(out=dst, in_=src)
 
-        def w_copy(h, t):
-            if t == 0:
-                w_alloc(h)
-            dst, src = w_views(h, t, t + W_SLICES)
+        def w_copy(h):
+            w_alloc(h)
+            dst, src = w_views(h, 0, PACK)
             nc.vector.tensor_copy(out=dst, in_=src)
 
         def w_quant(h):
@@ -140,19 +139,6 @@ def tile_multiheadattention_pa_kernel(tc, x, w, out):
         o_sb = {}
         banks = {}
         accs = {}
-        reads = [0]
-
-        def psum_read(dst, src):
-            n = reads[0]
-            reads[0] = n + 1
-            if n < TAIL_FROM:
-                on_scalar = ((n + 1) * SCALAR_NUM) // SCALAR_DEN != (n * SCALAR_NUM) // SCALAR_DEN
-            else:
-                on_scalar = (n - TAIL_FROM) % 2 == 1
-            if on_scalar:
-                nc.scalar.copy(out=dst, in_=src)
-            else:
-                nc.vector.tensor_copy(out=dst, in_=src)
 
         def stage1(h, i):
             if i == 0:
@@ -162,8 +148,8 @@ def tile_multiheadattention_pa_kernel(tc, x, w, out):
                 xs_grouped[h] = xg
                 xs_codes[h] = xc
                 xs_scales[h] = xsc
-            bank = psum.tile([P, PACK, P], BANK_DT, name="bank", tag="s1")
-            cols = slice(i * P, (i + 1) * P)
+            bank = psum.tile([P, PACK, PAIR * P], BANK_DT, name="bank", tag="s1")
+            cols = slice(i * PAIR * P, (i + 1) * PAIR * P)
             for t in range(PACK):
                 chans = slice(t * P, (t + 1) * P)
                 nc.tensor.matmul_mx(
@@ -178,10 +164,13 @@ def tile_multiheadattention_pa_kernel(tc, x, w, out):
             banks[(h, i)] = bank
 
         def read_bank(h, i):
-            psum_read(xs_grouped[h][:, i * P : (i + 1) * P, :], banks[(h, i)][:].rearrange("p t l -> p l t"))
+            nc.scalar.copy(
+                out=xs_grouped[h][:, i * PAIR * P : (i + 1) * PAIR * P, :],
+                in_=banks[(h, i)][:].rearrange("p t l -> p l t"),
+            )
 
         def xs_quant(h, k):
-            cols = slice(k * QC * P, (k + 1) * QC * P)
+            cols = slice(k * QP * PAIR * P, (k + 1) * QP * PAIR * P)
             nc.vector.quantize_mx(
                 out=xs_codes[h][:, cols].bitcast(FP8X4),
                 scales=xs_scales[h][:, cols],
@@ -206,10 +195,17 @@ def tile_multiheadattention_pa_kernel(tc, x, w, out):
             accs[(h, i)] = acc
 
         def read_acc(h, i):
-            psum_read(
-                o_sb[h][:, i, :].rearrange("p (m t) -> p m t", t=PACK),
-                accs[(h, i)][:].rearrange("p (t m) -> p m t", t=PACK),
-            )
+            n = h * LT + i
+            if n < TAIL_FROM:
+                on_scalar = ((n + 1) * SCALAR_NUM) // SCALAR_DEN != (n * SCALAR_NUM) // SCALAR_DEN
+            else:
+                on_scalar = (n - TAIL_FROM) % 2 == 0
+            dst = o_sb[h][:, i, :].rearrange("p (m t) -> p m t", t=PACK)
+            src = accs[(h, i)][:].rearrange("p (t m) -> p m t", t=PACK)
+            if on_scalar:
+                nc.scalar.copy(out=dst, in_=src)
+            else:
+                nc.vector.tensor_copy(out=dst, in_=src)
 
         def store(h, a0, a1):
             nc.sync.dma_start(
@@ -227,34 +223,31 @@ def tile_multiheadattention_pa_kernel(tc, x, w, out):
             x_transpose(1)
             x_quant(2, 4)
 
-            for g in range(H * LT + SKEW):
+            for g in range(NP + SKEW):
                 g2 = g - SKEW
-                if g < H * LT:
-                    stage1(g // LT, g % LT)
+                if g < NP:
+                    stage1(g // HP, g % HP)
                 if g2 >= 0:
-                    stage2(g2 // LT, g2 % LT)
+                    for e in range(PAIR):
+                        stage2(g2 // HP, PAIR * (g2 % HP) + e)
                 if g == 0:
                     x_transpose(2)
                     x_transpose(3)
-                if g < H * LT:
-                    read_bank(g // LT, g % LT)
+                if g < NP:
+                    read_bank(g // HP, g % HP)
                 if g2 >= 0:
-                    read_acc(g2 // LT, g2 % LT)
+                    for e in range(PAIR):
+                        read_acc(g2 // HP, PAIR * (g2 % HP) + e)
+                        if g2 // HP == H - 1 and PAIR * (g2 % HP) + e in LAST_STORES:
+                            store(H - 1, LAST_STORES[PAIR * (g2 % HP) + e], PAIR * (g2 % HP) + e + 1)
+                    if g2 // HP < H - 1:
+                        store(g2 // HP, PAIR * (g2 % HP), PAIR * (g2 % HP) + PAIR)
                 if g == 1:
                     x_quant(4, 8)
-                gq = g - DQ
-                if 0 <= gq < H * LT and gq % QC == QC - 1:
-                    xs_quant(gq // LT, (gq % LT) // QC)
+                if g < NP and g % QP == QP - 1:
+                    xs_quant(g // HP, (g % HP) // QP)
                 for h in range(1, H):
-                    for t in range(0, PACK, W_SLICES):
-                        if g == max(t, LT * h - W_COPY_AHEAD + t):
-                            w_copy(h, t)
-                    if g == max(5, LT * h - W_QUANT_AHEAD):
+                    if g == max(0, HP * h - W_COPY_AHEAD):
+                        w_copy(h)
+                    if g == max(2, HP * h - W_QUANT_AHEAD):
                         w_quant(h)
-                if g2 >= 0:
-                    h2, i2 = g2 // LT, g2 % LT
-                    if h2 < H - 1:
-                        if i2 % STORE_CHUNKS == STORE_CHUNKS - 1:
-                            store(h2, i2 + 1 - STORE_CHUNKS, i2 + 1)
-                    elif i2 in LAST_STORES:
-                        store(h2, LAST_STORES[i2], i2 + 1)

@@ -24,8 +24,9 @@ SKEW = 3
 QP = 2
 SCALAR_NUM, SCALAR_DEN = 5, 16
 TAIL_FROM = H * LT - PAIR * SKEW
-W_COPY_AHEAD = 5
-W_QUANT_AHEAD = 2
+HALF = 2
+GP_FROM = 3
+W_QUANT_AHEAD = 5
 LAST_STORES = {1: 0, 3: 2, 5: 4, 6: 6, 7: 7}
 
 
@@ -38,7 +39,7 @@ def tile_multiheadattention_pa_kernel(tc, x, w, out):
     with ExitStack() as ctx:
         consts = ctx.enter_context(tc.tile_pool(name="consts", bufs=1))
         w_pool = ctx.enter_context(tc.tile_pool(name="w_pool", bufs=H))
-        wg_pool = ctx.enter_context(tc.tile_pool(name="wg_pool", bufs=2))
+        wg_pool = ctx.enter_context(tc.tile_pool(name="wg_pool", bufs=1))
         xs_pool = ctx.enter_context(tc.tile_pool(name="xs_pool", bufs=3))
         o_pool = ctx.enter_context(tc.tile_pool(name="o_pool", bufs=3))
         psum = ctx.enter_context(tc.psum_pool(name="psum", bufs=4))
@@ -80,35 +81,50 @@ def tile_multiheadattention_pa_kernel(tc, x, w, out):
         w_codes = {}
         w_scales = {}
 
-        def w_views(h, t0, t1):
-            dst = w_grouped[h][:, t0 * P * PACK : t1 * P * PACK].rearrange("p (t m j) -> p m j t", t=t1 - t0, j=PACK)
-            src = w_raw[h][:].rearrange("p j (m t) -> p m j t", t=PACK)[:, :, :, t0:t1]
+        def w_alloc(h, half):
+            wg = wg_pool.tile([P, HALF * P * PACK], BF16, name="wg", tag="wg%d" % half, align_bytes=64)
+            w_grouped[(h, half)] = wg
+
+        def w_views(h, t0, t1, order):
+            half = t0 // HALF
+            lo = (t0 - half * HALF) * P * PACK
+            hi = (t1 - half * HALF) * P * PACK
+            dst = w_grouped[(h, half)][:, lo:hi].rearrange("p (t m j) -> " + order, t=t1 - t0, j=PACK)
+            src = w_raw[h][:].rearrange("p j (m t) -> p t m j", t=PACK)[:, t0:t1, :, :].rearrange("p t m j -> " + order)
             return dst, src
 
-        def w_alloc(h):
-            wg = wg_pool.tile([P, D * PACK], BF16, name="wg", tag="wg", align_bytes=64)
-            w_grouped[h] = wg
-
         def w_copy_first():
-            w_alloc(0)
-            dst, src = w_views(0, 0, 2)
+            w_alloc(0, 0)
+            w_alloc(0, 1)
+            dst, src = w_views(0, 0, 2, "p m j t")
             nc.vector.tensor_copy(out=dst, in_=src)
-            dst, src = w_views(0, 3, 4)
+            dst, src = w_views(0, 3, 4, "p m j t")
             nc.scalar.copy(out=dst, in_=src)
-            dst, src = w_views(0, 2, 3)
+            dst, src = w_views(0, 2, 3, "p m j t")
             nc.vector.tensor_copy(out=dst, in_=src)
 
-        def w_copy(h):
-            w_alloc(h)
-            dst, src = w_views(h, 0, PACK)
+        def w_copy_vector(h, half):
+            w_alloc(h, half)
+            dst, src = w_views(h, half * HALF, (half + 1) * HALF, "p m j t")
             nc.vector.tensor_copy(out=dst, in_=src)
 
-        def w_quant(h):
-            wc = w_pool.tile([P, D], U32, name="wc", tag="w_codes", align_bytes=64)
-            ws = w_pool.tile([P, D], U8, name="ws", tag="w_scales", align_bytes=64)
-            nc.vector.quantize_mx(out=wc[:].bitcast(FP8X4), scales=ws[:], in_=w_grouped[h][:])
-            w_codes[h] = wc
-            w_scales[h] = ws
+        def w_copy_gpsimd(h, half):
+            w_alloc(h, half)
+            dst, src = w_views(h, half * HALF, (half + 1) * HALF, "p m j t")
+            nc.gpsimd.tensor_scalar(
+                out=dst, in0=src, scalar1=1.0, scalar2=0.0, op0=mybir.AluOpType.mult, op1=mybir.AluOpType.add
+            )
+
+        def w_quant(h, half):
+            if half == 0:
+                wc = w_pool.tile([P, D], U32, name="wc", tag="w_codes", align_bytes=64)
+                ws = w_pool.tile([P, D], U8, name="ws", tag="w_scales", align_bytes=64)
+                w_codes[h] = wc
+                w_scales[h] = ws
+            cols = slice(half * HALF * P, (half + 1) * HALF * P)
+            nc.vector.quantize_mx(
+                out=w_codes[h][:, cols].bitcast(FP8X4), scales=w_scales[h][:, cols], in_=w_grouped[(h, half)][:]
+            )
 
         x_grouped = consts.tile([P, LT, P, PACK], BF16, name="x_grouped", align_bytes=64)
         x_codes = consts.tile([P, L], U32, name="x_codes", align_bytes=64)
@@ -218,7 +234,8 @@ def tile_multiheadattention_pa_kernel(tc, x, w, out):
         with tc.manual_schedule():
             w_copy_first()
             x_transpose(0)
-            w_quant(0)
+            w_quant(0, 0)
+            w_quant(0, 1)
             x_quant(0, 2)
             x_transpose(1)
             x_quant(2, 4)
@@ -246,8 +263,19 @@ def tile_multiheadattention_pa_kernel(tc, x, w, out):
                     x_quant(4, 8)
                 if g < NP and g % QP == QP - 1:
                     xs_quant(g // HP, (g % HP) // QP)
-                for h in range(1, H):
-                    if g == max(0, HP * h - W_COPY_AHEAD):
-                        w_copy(h)
-                    if g == max(2, HP * h - W_QUANT_AHEAD):
-                        w_quant(h)
+                if g == 0:
+                    w_copy_vector(1, 0)
+                    w_copy_vector(1, 1)
+                if g == 1:
+                    w_quant(1, 0)
+                if g == 2:
+                    w_quant(1, 1)
+                    w_copy_vector(2, 0)
+                if g == 3:
+                    w_copy_vector(2, 1)
+                for h in range(2, H):
+                    for half in range(2):
+                        if g == HP * h - W_QUANT_AHEAD + QP * half:
+                            w_quant(h, half)
+                            if h + 1 >= GP_FROM and h + 1 < H:
+                                w_copy_gpsimd(h + 1, half)

@@ -22,7 +22,7 @@ NP = H * LT // PAIR
 HP = LT // PAIR
 SKEW = 3
 QP = 2
-SCALAR_NUM, SCALAR_DEN = 5, 16
+SCALAR_NUM, SCALAR_DEN = 1, 4
 TAIL_FROM = H * LT - PAIR * SKEW
 HALF = 2
 GP_FROM = 3

@@ -26,6 +26,8 @@ SCALAR_NUM, SCALAR_DEN = 1, 4
 TAIL_FROM = H * LT - PAIR * SKEW
 HALF = 2
 GP_FROM = 3
+WARM_FIRST = 8
+WARM_MORE = 2
 W_QUANT_AHEAD = 5
 LAST_STORES = {1: 0, 3: 2, 5: 4, 6: 6, 7: 7}
 
@@ -48,6 +50,9 @@ def tile_multiheadattention_pa_kernel(tc, x, w, out):
         warm_out = consts.tile([P, 1], F32, name="warm_out")
         nc.vector.memset(warm_in[:], 0.0)
         nc.scalar.copy(out=warm_out[:], in_=warm_in[:])
+
+        pe_warm = consts.tile([P, D], BF16, name="pe_warm")
+        nc.vector.memset(pe_warm[:], 0.0)
 
         ident = consts.tile([P, P], F32, name="ident")
         make_identity(nc, ident[:])
@@ -180,10 +185,16 @@ def tile_multiheadattention_pa_kernel(tc, x, w, out):
             banks[(h, i)] = bank
 
         def read_bank(h, i):
-            nc.scalar.copy(
-                out=xs_grouped[h][:, i * PAIR * P : (i + 1) * PAIR * P, :],
-                in_=banks[(h, i)][:].rearrange("p t l -> p l t"),
-            )
+            dst = xs_grouped[h][:, i * PAIR * P : (i + 1) * PAIR * P, :]
+            src = banks[(h, i)][:].rearrange("p t l -> p l t")
+            if h == 0 and i == 0:
+                nc.vector.tensor_copy(out=dst, in_=src)
+            else:
+                nc.scalar.copy(out=dst, in_=src)
+
+        def warm_up(n):
+            for k in range(n):
+                nc.tensor.matmul(out=warm_acc[:], lhsT=pe_warm[:, 0:P], rhs=pe_warm[:], start=True, stop=True)
 
         def xs_quant(h, k):
             cols = slice(k * QP * PAIR * P, (k + 1) * QP * PAIR * P)
@@ -232,8 +243,11 @@ def tile_multiheadattention_pa_kernel(tc, x, w, out):
             )
 
         with tc.manual_schedule():
+            warm_acc = psum.tile([P, D], F32, name="warm_acc", tag="s2")
+            warm_up(WARM_FIRST)
             w_copy_first()
             x_transpose(0)
+            warm_up(WARM_MORE)
             w_quant(0, 0)
             w_quant(0, 1)
             x_quant(0, 2)

@@ -278,13 +278,12 @@ def tile_multiheadattention_pa_kernel(tc, x, w, out):
                 if g < NP and g % QP == QP - 1:
                     xs_quant(g // HP, (g % HP) // QP)
                 if g == 0:
+                    w_copy_gpsimd(1, 1)
                     w_copy_vector(1, 0)
-                    w_copy_vector(1, 1)
                 if g == 1:
                     w_quant(1, 0)
-                if g == 2:
                     w_quant(1, 1)
-                    w_copy_vector(2, 0)
+                    w_copy_gpsimd(2, 0)
                 if g == 3:
                     w_copy_vector(2, 1)
                 for h in range(2, H):

@@ -135,15 +135,20 @@ def tile_multiheadattention_pa_kernel(tc, x, w, out):
         x_codes = consts.tile([P, L], U32, name="x_codes", align_bytes=64)
         x_scales = consts.tile([P, L], U8, name="x_scales", align_bytes=64)
 
+        x_turned = {}
+
         def x_transpose(pr):
             xt = psum.tile([P, 2, 2, P], F32, name="xt", tag="s1")
+            x_turned[pr] = xt
             for a2 in range(2):
                 words = x_sb[:, 2 * pr + a2, :].bitcast(F32)
                 for u in range(2):
                     nc.tensor.transpose(xt[:, a2, u, :], words[:, u : D // 2 : 2], ident[:])
+
+        def x_copy(pr):
             nc.scalar.copy(
                 out=x_grouped[:, 2 * pr : 2 * pr + 2, :, :].bitcast(F32),
-                in_=xt[:].rearrange("p a u r -> p a r u"),
+                in_=x_turned[pr][:].rearrange("p a u r -> p a r u"),
             )
 
         def x_quant(a0, a1):
@@ -187,10 +192,7 @@ def tile_multiheadattention_pa_kernel(tc, x, w, out):
         def read_bank(h, i):
             dst = xs_grouped[h][:, i * PAIR * P : (i + 1) * PAIR * P, :]
             src = banks[(h, i)][:].rearrange("p t l -> p l t")
-            if h == 0 and i == 0:
-                nc.vector.tensor_copy(out=dst, in_=src)
-            else:
-                nc.scalar.copy(out=dst, in_=src)
+            nc.scalar.copy(out=dst, in_=src)
 
         def warm_up(n):
             for k in range(n):
@@ -247,11 +249,17 @@ def tile_multiheadattention_pa_kernel(tc, x, w, out):
             warm_up(WARM_FIRST)
             w_copy_first()
             x_transpose(0)
+            x_copy(0)
+            x_transpose(1)
+            x_copy(1)
             warm_up(WARM_MORE)
             w_quant(0, 0)
             w_quant(0, 1)
             x_quant(0, 2)
-            x_transpose(1)
+            x_transpose(2)
+            x_copy(2)
+            x_transpose(3)
+            x_copy(3)
             x_quant(2, 4)
 
             for g in range(NP + SKEW):
@@ -261,9 +269,6 @@ def tile_multiheadattention_pa_kernel(tc, x, w, out):
                 if g2 >= 0:
                     for e in range(PAIR):
                         stage2(g2 // HP, PAIR * (g2 % HP) + e)
-                if g == 0:
-                    x_transpose(2)
-                    x_transpose(3)
                 if g < NP:
                     read_bank(g // HP, g % HP)
                 if g2 >= 0:
@@ -273,22 +278,23 @@ def tile_multiheadattention_pa_kernel(tc, x, w, out):
                             store(H - 1, LAST_STORES[PAIR * (g2 % HP) + e], PAIR * (g2 % HP) + e + 1)
                     if g2 // HP < H - 1:
                         store(g2 // HP, PAIR * (g2 % HP), PAIR * (g2 % HP) + PAIR)
+                if g == 0:
+                    w_copy_vector(1, 0)
+                    w_copy_vector(1, 1)
                 if g == 1:
-                    x_quant(4, 8)
+                    x_quant(4, 6)
+                    w_quant(1, 0)
+                    x_quant(6, 8)
                 if g < NP and g % QP == QP - 1:
                     xs_quant(g // HP, (g % HP) // QP)
-                if g == 0:
-                    w_copy_gpsimd(1, 1)
-                    w_copy_vector(1, 0)
                 if g == 1:
-                    w_quant(1, 0)
                     w_quant(1, 1)
-                    w_copy_gpsimd(2, 0)
-                if g == 3:
-                    w_copy_vector(2, 1)
+                    w_copy_vector(2, 0)
                 for h in range(2, H):
                     for half in range(2):
                         if g == HP * h - W_QUANT_AHEAD + QP * half:
                             w_quant(h, half)
+                            if h == 2 and half == 0:
+                                w_copy_gpsimd(2, 1)
                             if h + 1 >= GP_FROM and h + 1 < H:
                                 w_copy_gpsimd(h + 1, half)

@@ -29,6 +29,7 @@ GP_FROM = 3
 WARM_FIRST = 8
 WARM_MORE = 2
 W_QUANT_AHEAD = 5
+X_PAIR_ON_VECTOR = 2
 LAST_STORES = {1: 0, 3: 2, 5: 4, 6: 6, 7: 7}
 
 
@@ -146,10 +147,12 @@ def tile_multiheadattention_pa_kernel(tc, x, w, out):
                     nc.tensor.transpose(xt[:, a2, u, :], words[:, u : D // 2 : 2], ident[:])
 
         def x_copy(pr):
-            nc.scalar.copy(
-                out=x_grouped[:, 2 * pr : 2 * pr + 2, :, :].bitcast(F32),
-                in_=x_turned[pr][:].rearrange("p a u r -> p a r u"),
-            )
+            dst = x_grouped[:, 2 * pr : 2 * pr + 2, :, :].bitcast(F32)
+            src = x_turned[pr][:].rearrange("p a u r -> p a r u")
+            if pr == X_PAIR_ON_VECTOR:
+                nc.vector.tensor_copy(out=dst, in_=src)
+            else:
+                nc.scalar.copy(out=dst, in_=src)
 
         def x_quant(a0, a1):
             cols = slice(P * a0, P * a1)
@@ -198,8 +201,8 @@ def tile_multiheadattention_pa_kernel(tc, x, w, out):
             for k in range(n):
                 nc.tensor.matmul(out=warm_acc[:], lhsT=pe_warm[:, 0:P], rhs=pe_warm[:], start=True, stop=True)
 
-        def xs_quant(h, k):
-            cols = slice(k * QP * PAIR * P, (k + 1) * QP * PAIR * P)
+        def xs_quant(h, i0, i1):
+            cols = slice(i0 * PAIR * P, i1 * PAIR * P)
             nc.vector.quantize_mx(
                 out=xs_codes[h][:, cols].bitcast(FP8X4),
                 scales=xs_scales[h][:, cols],
@@ -256,11 +259,11 @@ def tile_multiheadattention_pa_kernel(tc, x, w, out):
             w_quant(0, 0)
             w_quant(0, 1)
             x_quant(0, 2)
+            x_quant(2, 4)
             x_transpose(2)
-            x_copy(2)
             x_transpose(3)
             x_copy(3)
-            x_quant(2, 4)
+            x_copy(2)
 
             for g in range(NP + SKEW):
                 g2 = g - SKEW
@@ -279,17 +282,19 @@ def tile_multiheadattention_pa_kernel(tc, x, w, out):
                     if g2 // HP < H - 1:
                         store(g2 // HP, PAIR * (g2 % HP), PAIR * (g2 % HP) + PAIR)
                 if g == 0:
-                    w_copy_vector(1, 0)
                     w_copy_vector(1, 1)
-                if g == 1:
                     x_quant(4, 6)
-                    w_quant(1, 0)
-                    x_quant(6, 8)
-                if g < NP and g % QP == QP - 1:
-                    xs_quant(g // HP, (g % HP) // QP)
+                    w_copy_vector(1, 0)
                 if g == 1:
-                    w_quant(1, 1)
+                    x_quant(6, 8)
+                    w_quant(1, 0)
+                    xs_quant(0, 0, 1)
                     w_copy_vector(2, 0)
+                    w_quant(1, 1)
+                if g == 2:
+                    xs_quant(0, 1, 2)
+                if g > 2 and g < NP and g % QP == QP - 1:
+                    xs_quant(g // HP, g % HP - QP + 1, g % HP + 1)
                 for h in range(2, H):
                     for half in range(2):
                         if g == HP * h - W_QUANT_AHEAD + QP * half:

@@ -25,7 +25,7 @@ QP = 2
 SCALAR_NUM, SCALAR_DEN = 1, 4
 TAIL_FROM = H * LT - PAIR * SKEW
 HALF = 2
-GP_FROM = 3
+GP_FROM = 2
 WARM_FIRST = 8
 WARM_MORE = 2
 W_QUANT_AHEAD = 5
@@ -88,7 +88,7 @@ def tile_multiheadattention_pa_kernel(tc, x, w, out):
         w_scales = {}
 
         def w_alloc(h, half):
-            wg = wg_pool.tile([P, HALF * P * PACK], BF16, name="wg", tag="wg%d" % half, align_bytes=64)
+            wg = wg_pool.tile([P, HALF * P * PACK], BF16, name="wg", tag="wg%d" % (half if h < GP_FROM else 1), align_bytes=64)
             w_grouped[(h, half)] = wg
 
         def w_views(h, t0, t1, order):
@@ -289,8 +289,8 @@ def tile_multiheadattention_pa_kernel(tc, x, w, out):
                     x_quant(6, 8)
                     w_quant(1, 0)
                     xs_quant(0, 0, 1)
-                    w_copy_vector(2, 0)
                     w_quant(1, 1)
+                    w_copy_gpsimd(2, 0)
                 if g == 2:
                     xs_quant(0, 1, 2)
                 if g > 2 and g < NP and g % QP == QP - 1:
@@ -299,7 +299,7 @@ def tile_multiheadattention_pa_kernel(tc, x, w, out):
                     for half in range(2):
                         if g == HP * h - W_QUANT_AHEAD + QP * half:
                             w_quant(h, half)
-                            if h == 2 and half == 0:
-                                w_copy_gpsimd(2, 1)
-                            if h + 1 >= GP_FROM and h + 1 < H:
-                                w_copy_gpsimd(h + 1, half)
+                            if half == 0:
+                                w_copy_gpsimd(h, 1)
+                            elif h + 1 < H:
+                                w_copy_gpsimd(h + 1, 0)

@@ -21,6 +21,8 @@ PAIR = 2
 NP = H * LT // PAIR
 HP = LT // PAIR
 SKEW = 3
+CATCH_UP = 28
+SINGLE_FROM = 26
 QP = 2
 SCALAR_NUM, SCALAR_DEN = 1, 4
 TAIL_FROM = H * LT - PAIR * SKEW
@@ -30,7 +32,7 @@ WARM_FIRST = 8
 WARM_MORE = 2
 W_QUANT_AHEAD = 5
 X_PAIR_ON_VECTOR = 2
-LAST_STORES = {1: 0, 3: 2, 5: 4, 6: 6, 7: 7}
+LAST_STORES = {1: 0, 3: 2, 5: 4, 7: 6}
 
 
 def tile_multiheadattention_pa_kernel(tc, x, w, out):
@@ -229,7 +231,7 @@ def tile_multiheadattention_pa_kernel(tc, x, w, out):
         def read_acc(h, i):
             n = h * LT + i
             if n < TAIL_FROM:
-                on_scalar = ((n + 1) * SCALAR_NUM) // SCALAR_DEN != (n * SCALAR_NUM) // SCALAR_DEN
+                on_scalar = n % 4 == 3
             else:
                 on_scalar = (n - TAIL_FROM) % 2 == 0
             dst = o_sb[h][:, i, :].rearrange("p (m t) -> p m t", t=PACK)
@@ -265,16 +267,22 @@ def tile_multiheadattention_pa_kernel(tc, x, w, out):
             x_copy(3)
             x_copy(2)
 
-            for g in range(NP + SKEW):
-                g2 = g - SKEW
+            for g in range(NP + SKEW - 1):
+                if g < CATCH_UP:
+                    pairs = [g - SKEW]
+                elif g == CATCH_UP:
+                    pairs = [g - SKEW, g - SKEW + 1]
+                else:
+                    pairs = [g - SKEW + 1]
+                pairs = [q for q in pairs if q >= 0]
                 if g < NP:
                     stage1(g // HP, g % HP)
-                if g2 >= 0:
+                for g2 in pairs:
                     for e in range(PAIR):
                         stage2(g2 // HP, PAIR * (g2 % HP) + e)
                 if g < NP:
                     read_bank(g // HP, g % HP)
-                if g2 >= 0:
+                for g2 in pairs:
                     for e in range(PAIR):
                         read_acc(g2 // HP, PAIR * (g2 % HP) + e)
                         if g2 // HP == H - 1 and PAIR * (g2 % HP) + e in LAST_STORES:
@@ -293,8 +301,10 @@ def tile_multiheadattention_pa_kernel(tc, x, w, out):
                     w_copy_gpsimd(2, 0)
                 if g == 2:
                     xs_quant(0, 1, 2)
-                if g > 2 and g < NP and g % QP == QP - 1:
+                if g > 2 and g < SINGLE_FROM and g % QP == QP - 1:
                     xs_quant(g // HP, g % HP - QP + 1, g % HP + 1)
+                if g >= SINGLE_FROM and g < NP:
+                    xs_quant(g // HP, g % HP, g % HP + 1)
                 for h in range(2, H):
                     for half in range(2):
                         if g == HP * h - W_QUANT_AHEAD + QP * half:

@@ -302,7 +302,8 @@ def tile_multiheadattention_pa_kernel(tc, x, w, out):
                 if g == 2:
                     xs_quant(0, 1, 2)
                 if g > 2 and g < SINGLE_FROM and g % QP == QP - 1:
-                    xs_quant(g // HP, g % HP - QP + 1, g % HP + 1)
+                    xs_quant(g // HP, g % HP - 1, g % HP)
+                    xs_quant(g // HP, g % HP, g % HP + 1)
                 if g >= SINGLE_FROM and g < NP:
                     xs_quant(g // HP, g % HP, g % HP + 1)
                 for h in range(2, H):

@@ -303,7 +303,6 @@ def tile_multiheadattention_pa_kernel(tc, x, w, out):
                     xs_quant(0, 1, 2)
                 if g > 2 and g < SINGLE_FROM and g % QP == QP - 1:
                     xs_quant(g // HP, g % HP - 1, g % HP)
-                    xs_quant(g // HP, g % HP, g % HP + 1)
                 if g >= SINGLE_FROM and g < NP:
                     xs_quant(g // HP, g % HP, g % HP + 1)
                 for h in range(2, H):
@@ -314,3 +313,5 @@ def tile_multiheadattention_pa_kernel(tc, x, w, out):
                                 w_copy_gpsimd(h, 1)
                             elif h + 1 < H:
                                 w_copy_gpsimd(h + 1, 0)
+                if g > 2 and g < SINGLE_FROM and g % QP == QP - 1:
+                    xs_quant(g // HP, g % HP, g % HP + 1)

@@ -141,7 +141,7 @@ def tile_multiheadattention_pa_kernel(tc, x, w, out):
         x_turned = {}
 
         def x_transpose(pr):
-            xt = psum.tile([P, 2, 2, P], F32, name="xt", tag="s1")
+            xt = psum.tile([P, 2, 2, P], F32, name="xt", tag="s1", bufs=3)
             x_turned[pr] = xt
             for a2 in range(2):
                 words = x_sb[:, 2 * pr + a2, :].bitcast(F32)
@@ -179,7 +179,7 @@ def tile_multiheadattention_pa_kernel(tc, x, w, out):
                 xs_grouped[h] = xg
                 xs_codes[h] = xc
                 xs_scales[h] = xsc
-            bank = psum.tile([P, PACK, PAIR * P], BANK_DT, name="bank", tag="s1")
+            bank = psum.tile([P, PACK, PAIR * P], BANK_DT, name="bank", tag="s1", bufs=3)
             cols = slice(i * PAIR * P, (i + 1) * PAIR * P)
             for t in range(PACK):
                 chans = slice(t * P, (t + 1) * P)
@@ -215,7 +215,7 @@ def tile_multiheadattention_pa_kernel(tc, x, w, out):
             if i == 0:
                 ot = o_pool.tile([P, LT, D], F32, name="ot", tag="o_sb")
                 o_sb[h] = ot
-            acc = psum.tile([P, D], F32, name="acc", tag="s2")
+            acc = psum.tile([P, D], F32, name="acc", tag="s2", bufs=5)
             cols = slice(i * P, (i + 1) * P)
             nc.tensor.matmul_mx(
                 out=acc[:],
@@ -250,7 +250,7 @@ def tile_multiheadattention_pa_kernel(tc, x, w, out):
             )
 
         with tc.manual_schedule():
-            warm_acc = psum.tile([P, D], F32, name="warm_acc", tag="s2")
+            warm_acc = psum.tile([P, D], F32, name="warm_acc", tag="s2", bufs=5)
             warm_up(WARM_FIRST)
             w_copy_first()
             x_transpose(0)

@@ -295,8 +295,8 @@ def tile_multiheadattention_pa_kernel(tc, x, w, out):
                     w_copy_vector(1, 0)
                 if g == 1:
                     x_quant(6, 8)
-                    w_quant(1, 0)
                     xs_quant(0, 0, 1)
+                    w_quant(1, 0)
                     w_quant(1, 1)
                     w_copy_gpsimd(2, 0)
                 if g == 2:

@@ -21,7 +21,7 @@ PAIR = 2
 NP = H * LT // PAIR
 HP = LT // PAIR
 SKEW = 3
-CATCH_UP = 28
+CATCH_UP = 27
 SINGLE_FROM = 26
 QP = 2
 SCALAR_NUM, SCALAR_DEN = 1, 4

from contextlib import ExitStack

import concourse.mybir as mybir
from concourse.masks import make_identity

H, L, D = 8, 1024, 512
FLOPS = 2 * 2 * H * L * D * D

F32 = mybir.dt.float32
BF16 = mybir.dt.bfloat16
U32 = mybir.dt.uint32
U8 = mybir.dt.uint8
FP8X4 = mybir.dt.float8_e4m3fn_x4

P = 128
PACK = 4
LT = L // P
BANK_DT = BF16

PAIR = 2
NP = H * LT // PAIR
HP = LT // PAIR
SKEW = 3
CATCH_UP = 27
SINGLE_FROM = 26
QP = 2
SCALAR_NUM, SCALAR_DEN = 1, 4
TAIL_FROM = H * LT - PAIR * SKEW
HALF = 2
GP_FROM = 2
WARM_FIRST = 8
WARM_MORE = 2
W_QUANT_AHEAD = 5
X_PAIR_ON_VECTOR = 2
LAST_STORES = {1: 0, 3: 2, 5: 4, 7: 6}


def tile_multiheadattention_pa_kernel(tc, x, w, out):
    nc = tc.nc
    x_rows = x.flatten_outer_dims().rearrange("(s p e) k -> p s e k", s=LT // 2, e=2)
    w_rows = w.flatten_outer_dims()
    out_rows = out.flatten_outer_dims()

    with ExitStack() as ctx:
        consts = ctx.enter_context(tc.tile_pool(name="consts", bufs=1))
        w_pool = ctx.enter_context(tc.tile_pool(name="w_pool", bufs=H))
        wg_pool = ctx.enter_context(tc.tile_pool(name="wg_pool", bufs=1))
        xs_pool = ctx.enter_context(tc.tile_pool(name="xs_pool", bufs=3))
        o_pool = ctx.enter_context(tc.tile_pool(name="o_pool", bufs=3))
        psum = ctx.enter_context(tc.psum_pool(name="psum", bufs=4))

        warm_in = consts.tile([P, 1], F32, name="warm_in")
        warm_out = consts.tile([P, 1], F32, name="warm_out")
        nc.vector.memset(warm_in[:], 0.0)
        nc.scalar.copy(out=warm_out[:], in_=warm_in[:])

        pe_warm = consts.tile([P, D], BF16, name="pe_warm")
        nc.vector.memset(pe_warm[:], 0.0)

        ident = consts.tile([P, P], F32, name="ident")
        make_identity(nc, ident[:])

        x_sb = consts.tile([P, LT, D], BF16, name="x_sb")
        w_raw = []
        for h in range(H):
            w_raw_h = w_pool.tile([P, PACK, D], BF16, name="w_raw_h", tag="w_raw")
            w_raw.append(w_raw_h)

        def load_x(a0, a1):
            nc.sync.dma_start(
                out=x_sb[:, a0:a1, :].rearrange("p (s e) k -> p s e k", e=2),
                in_=x_rows[:, a0 // 2 : a1 // 2, :, :],
            )

        def load_w(h):
            nc.sync.dma_start(
                out=w_raw[h][:],
                in_=w_rows[h * D : (h + 1) * D, :].rearrange("(p j) c -> p j c", j=PACK),
            )

        load_w(0)
        load_x(0, 2)
        load_x(2, 4)
        load_x(4, 8)
        for h in range(1, H):
            load_w(h)

        w_grouped = {}
        w_codes = {}
        w_scales = {}

        def w_alloc(h, half):
            wg = wg_pool.tile([P, HALF * P * PACK], BF16, name="wg", tag="wg%d" % (half if h < GP_FROM else 1), align_bytes=64)
            w_grouped[(h, half)] = wg

        def w_views(h, t0, t1, order):
            half = t0 // HALF
            lo = (t0 - half * HALF) * P * PACK
            hi = (t1 - half * HALF) * P * PACK
            dst = w_grouped[(h, half)][:, lo:hi].rearrange("p (t m j) -> " + order, t=t1 - t0, j=PACK)
            src = w_raw[h][:].rearrange("p j (m t) -> p t m j", t=PACK)[:, t0:t1, :, :].rearrange("p t m j -> " + order)
            return dst, src

        def w_copy_first():
            w_alloc(0, 0)
            w_alloc(0, 1)
            dst, src = w_views(0, 0, 2, "p m j t")
            nc.vector.tensor_copy(out=dst, in_=src)
            dst, src = w_views(0, 3, 4, "p m j t")
            nc.scalar.copy(out=dst, in_=src)
            dst, src = w_views(0, 2, 3, "p m j t")
            nc.vector.tensor_copy(out=dst, in_=src)

        def w_copy_vector(h, half):
            w_alloc(h, half)
            dst, src = w_views(h, half * HALF, (half + 1) * HALF, "p m j t")
            nc.vector.tensor_copy(out=dst, in_=src)

        def w_copy_gpsimd(h, half):
            w_alloc(h, half)
            dst, src = w_views(h, half * HALF, (half + 1) * HALF, "p m j t")
            nc.gpsimd.tensor_scalar(
                out=dst, in0=src, scalar1=1.0, scalar2=0.0, op0=mybir.AluOpType.mult, op1=mybir.AluOpType.add
            )

        def w_quant(h, half):
            if half == 0:
                wc = w_pool.tile([P, D], U32, name="wc", tag="w_codes", align_bytes=64)
                ws = w_pool.tile([P, D], U8, name="ws", tag="w_scales", align_bytes=64)
                w_codes[h] = wc
                w_scales[h] = ws
            cols = slice(half * HALF * P, (half + 1) * HALF * P)
            nc.vector.quantize_mx(
                out=w_codes[h][:, cols].bitcast(FP8X4), scales=w_scales[h][:, cols], in_=w_grouped[(h, half)][:]
            )

        x_grouped = consts.tile([P, LT, P, PACK], BF16, name="x_grouped", align_bytes=64)
        x_codes = consts.tile([P, L], U32, name="x_codes", align_bytes=64)
        x_scales = consts.tile([P, L], U8, name="x_scales", align_bytes=64)

        x_turned = {}

        def x_transpose(pr):
            xt = psum.tile([P, 2, 2, P], F32, name="xt", tag="s1", bufs=3)
            x_turned[pr] = xt
            for a2 in range(2):
                words = x_sb[:, 2 * pr + a2, :].bitcast(F32)
                for u in range(2):
                    nc.tensor.transpose(xt[:, a2, u, :], words[:, u : D // 2 : 2], ident[:])

        def x_copy(pr):
            dst = x_grouped[:, 2 * pr : 2 * pr + 2, :, :].bitcast(F32)
            src = x_turned[pr][:].rearrange("p a u r -> p a r u")
            if pr == X_PAIR_ON_VECTOR:
                nc.vector.tensor_copy(out=dst, in_=src)
            else:
                nc.scalar.copy(out=dst, in_=src)

        def x_quant(a0, a1):
            cols = slice(P * a0, P * a1)
            nc.vector.quantize_mx(
                out=x_codes[:, cols].bitcast(FP8X4),
                scales=x_scales[:, cols],
                in_=x_grouped[:, a0:a1, :, :].rearrange("p a r j -> p (a r j)"),
            )

        xs_grouped = {}
        xs_codes = {}
        xs_scales = {}
        o_sb = {}
        banks = {}
        accs = {}

        def stage1(h, i):
            if i == 0:
                xg = xs_pool.tile([P, L, PACK], BF16, name="xg", tag="xs_grouped", align_bytes=64)
                xc = xs_pool.tile([P, L], U32, name="xc", tag="xs_codes", align_bytes=64)
                xsc = xs_pool.tile([P, L], U8, name="xsc", tag="xs_scales", align_bytes=64)
                xs_grouped[h] = xg
                xs_codes[h] = xc
                xs_scales[h] = xsc
            bank = psum.tile([P, PACK, PAIR * P], BANK_DT, name="bank", tag="s1", bufs=3)
            cols = slice(i * PAIR * P, (i + 1) * PAIR * P)
            for t in range(PACK):
                chans = slice(t * P, (t + 1) * P)
                nc.tensor.matmul_mx(
                    out=bank[:, t, :],
                    lhsT=w_codes[h][:, chans].bitcast(FP8X4),
                    lhsT_scale=w_scales[h][:, chans],
                    rhs=x_codes[:, cols].bitcast(FP8X4),
                    rhs_scale=x_scales[:, cols],
                    start=True,
                    stop=True,
                )
            banks[(h, i)] = bank

        def read_bank(h, i):
            dst = xs_grouped[h][:, i * PAIR * P : (i + 1) * PAIR * P, :]
            src = banks[(h, i)][:].rearrange("p t l -> p l t")
            nc.scalar.copy(out=dst, in_=src)

        def warm_up(n):
            for k in range(n):
                nc.tensor.matmul(out=warm_acc[:], lhsT=pe_warm[:, 0:P], rhs=pe_warm[:], start=True, stop=True)

        def xs_quant(h, i0, i1):
            cols = slice(i0 * PAIR * P, i1 * PAIR * P)
            nc.vector.quantize_mx(
                out=xs_codes[h][:, cols].bitcast(FP8X4),
                scales=xs_scales[h][:, cols],
                in_=xs_grouped[h][:, cols, :].rearrange("p l j -> p (l j)"),
            )

        def stage2(h, i):
            if i == 0:
                ot = o_pool.tile([P, LT, D], F32, name="ot", tag="o_sb")
                o_sb[h] = ot
            acc = psum.tile([P, D], F32, name="acc", tag="s2", bufs=5)
            cols = slice(i * P, (i + 1) * P)
            nc.tensor.matmul_mx(
                out=acc[:],
                lhsT=xs_codes[h][:, cols].bitcast(FP8X4),
                lhsT_scale=xs_scales[h][:, cols],
                rhs=w_codes[h][:].bitcast(FP8X4),
                rhs_scale=w_scales[h][:],
                start=True,
                stop=True,
            )
            accs[(h, i)] = acc

        def read_acc(h, i):
            n = h * LT + i
            if n < TAIL_FROM:
                on_scalar = n % 4 == 3
            else:
                on_scalar = (n - TAIL_FROM) % 2 == 0
            dst = o_sb[h][:, i, :].rearrange("p (m t) -> p m t", t=PACK)
            src = accs[(h, i)][:].rearrange("p (t m) -> p m t", t=PACK)
            if on_scalar:
                nc.scalar.copy(out=dst, in_=src)
            else:
                nc.vector.tensor_copy(out=dst, in_=src)

        def store(h, a0, a1):
            nc.sync.dma_start(
                out=out_rows[h * L : (h + 1) * L, :].rearrange("(s p e) f -> p s e f", s=LT // 2, e=2)[
                    :, a0 // 2, a0 % 2 : a0 % 2 + a1 - a0, :
                ],
                in_=o_sb[h][:, a0:a1, :],
            )

        with tc.manual_schedule():
            warm_acc = psum.tile([P, D], F32, name="warm_acc", tag="s2", bufs=5)
            warm_up(WARM_FIRST)
            w_copy_first()
            x_transpose(0)
            x_copy(0)
            x_transpose(1)
            x_copy(1)
            warm_up(WARM_MORE)
            w_quant(0, 0)
            w_quant(0, 1)
            x_quant(0, 2)
            x_quant(2, 4)
            x_transpose(2)
            x_transpose(3)
            x_copy(3)
            x_copy(2)

            for g in range(NP + SKEW - 1):
                if g < CATCH_UP:
                    pairs = [g - SKEW]
                elif g == CATCH_UP:
                    pairs = [g - SKEW, g - SKEW + 1]
                else:
                    pairs = [g - SKEW + 1]
                pairs = [q for q in pairs if q >= 0]
                if g < NP:
                    stage1(g // HP, g % HP)
                for g2 in pairs:
                    for e in range(PAIR):
                        stage2(g2 // HP, PAIR * (g2 % HP) + e)
                if g < NP:
                    read_bank(g // HP, g % HP)
                for g2 in pairs:
                    for e in range(PAIR):
                        read_acc(g2 // HP, PAIR * (g2 % HP) + e)
                        if g2 // HP == H - 1 and PAIR * (g2 % HP) + e in LAST_STORES:
                            store(H - 1, LAST_STORES[PAIR * (g2 % HP) + e], PAIR * (g2 % HP) + e + 1)
                    if g2 // HP < H - 1:
                        store(g2 // HP, PAIR * (g2 % HP), PAIR * (g2 % HP) + PAIR)
                if g == 0:
                    w_copy_vector(1, 1)
                    x_quant(4, 6)
                    w_copy_vector(1, 0)
                if g == 1:
                    x_quant(6, 8)
                    xs_quant(0, 0, 1)
                    w_quant(1, 0)
                    w_quant(1, 1)
                    w_copy_gpsimd(2, 0)
                if g == 2:
                    xs_quant(0, 1, 2)
                if g > 2 and g < SINGLE_FROM and g % QP == QP - 1:
                    xs_quant(g // HP, g % HP - 1, g % HP)
                if g >= SINGLE_FROM and g < NP:
                    xs_quant(g // HP, g % HP, g % HP + 1)
                for h in range(2, H):
                    for half in range(2):
                        if g == HP * h - W_QUANT_AHEAD + QP * half:
                            w_quant(h, half)
                            if half == 0:
                                w_copy_gpsimd(h, 1)
                            elif h + 1 < H:
                                w_copy_gpsimd(h + 1, 0)
                if g > 2 and g < SINGLE_FROM and g % QP == QP - 1:
                    xs_quant(g // HP, g % HP, g % HP + 1)
